import numpy as np
import ml_dtypes


def mxq(x, axis, fmt="e4m3"):
    dtype, down = {"e4m3": (ml_dtypes.float8_e4m3fn, 7), "e5m2": (ml_dtypes.float8_e5m2, 14)}[fmt]
    v = np.moveaxis(np.asarray(x, np.float32).astype(ml_dtypes.bfloat16).astype(np.float64), axis, -1)
    blocks = v.reshape(v.shape[:-1] + (-1, 32))
    amax = np.abs(blocks).max(-1, keepdims=True)
    byte = np.maximum(np.where(amax > 0, np.frexp(amax)[1] - 1 + 127, 0) - down, 1)
    scale = np.exp2(byte - 127.0)
    codes = (blocks / scale).astype(np.float32).astype(dtype).astype(np.float64)
    return np.moveaxis((codes * scale).reshape(v.shape), -1, axis)


WIDE = False


def mx_kscale(k):
    if not WIDE:
        return np.ones(k)
    levels = np.array([10, -10, 5, -5, 0])
    if k % 512:
        return np.exp2(np.random.permutation(np.resize(levels, k // 32))).repeat(32)
    a = np.empty((k // 512, 16))
    for p in range(k // 512):
        a[p, :8] = np.random.permutation(np.resize(levels, 8))
        for g in range(8):
            far = levels[np.abs(levels - a[p, g]) >= 10]
            a[p, g + 8] = far[np.random.randint(len(far))]
    return np.exp2(a.ravel()).repeat(32)


BF16 = ml_dtypes.bfloat16


def bf(x):
    return np.asarray(x, np.float32).astype(BF16)


def f64(x):
    return np.asarray(x).astype(np.float64)


B, T, L, DM, DC, A, H = 2, 512, 2048, 1024, 512, 512, 4
HD = A // H
ROPE_GAMMA = 10.0


def apply_rope(xh, cos, sin):
    d2 = xh.shape[-1] // 2
    x1, x2 = xh[..., :d2], xh[..., d2:]
    return np.concatenate([x1 * cos - x2 * sin, x1 * sin + x2 * cos], axis=-1)


def prefix_mask(n):
    lens = np.random.randint(n // 2, n, size=B)
    return bf(np.where(np.arange(n)[None, None, :] < lens[:, None, None], 1.0, 0.0))


def setup_inputs():
    s = mx_kscale(DM)
    return {"x": bf(np.random.standard_normal((B, DM, T)) * s[None, :, None]),
            "x_mask": prefix_mask(T),
            "Wq": bf(np.random.standard_normal((A, DM)) * 2.5 / np.sqrt(DM) / s[None, :]),
            "bq": bf(np.random.standard_normal(A) * 0.3)}


def core(x, x_mask, Wq, bq):
    xq = mxq(f64(x), 1, "e4m3")
    q = (xq.transpose(0, 2, 1) @ mxq(f64(Wq), 1, "e4m3").T) + f64(bq)
    q = q.reshape(B, T, H, HD).transpose(2, 0, 1, 3)
    len_q = f64(x_mask).sum(axis=(-2, -1)).reshape(-1, 1, 1)
    pos_q = np.arange(T, dtype=np.float64).reshape(1, -1, 1)
    theta = (ROPE_GAMMA / (10000.0 ** (np.arange(0, HD, 2, dtype=np.float64) / HD))).reshape(1, 1, -1)
    fq = pos_q / len_q * theta
    return apply_rope(q, np.cos(fq)[None], np.sin(fq)[None])


def e4m3fn_bytes(y):
    return np.clip(np.asarray(y, np.float64), -448.0, 448.0).astype(np.float32).astype(ml_dtypes.float8_e4m3fn).view(np.uint8)


def reference(x, x_mask, Wq, bq):
    out = core(x, x_mask, Wq, bq)
    s = np.max(np.abs(out), axis=-1, keepdims=True) / 448.0
    return out, e4m3fn_bytes(out / s)

@@ -1,0 +1,430 @@
+import math
+from contextlib import ExitStack
+
+import concourse.mybir as mybir
+from concourse.masks import make_identity
+
+B, T, DM, A, H, HD = 2, 512, 1024, 512, 4, 128
+FLOPS = 2 * B * T * DM * A
+
+F32 = mybir.dt.float32
+BF16 = mybir.dt.bfloat16
+I32 = mybir.dt.int32
+U32 = mybir.dt.uint32
+U8 = mybir.dt.uint8
+FP8X4 = mybir.dt.float8_e4m3fn_x4
+FP8 = mybir.dt.float8_e4m3fn
+ALU = mybir.AluOpType
+ACT = mybir.ActivationFunctionType
+AX = mybir.AxisListType
+
+P = 128
+TWO_PI = 2.0 * math.pi
+THETA0_TURNS = 10.0 / TWO_PI
+THETA_RATIO = 10000.0 ** (-2.0 / HD)
+
+
+def tile_attentionmodule_pa_kernel(tc, x, x_mask, Wq, bq, out_0, out_1):
+    nc = tc.nc
+    with ExitStack() as ctx:
+        keep = ctx.enter_context(tc.tile_pool(name="keep", bufs=1))
+        ps_acc = ctx.enter_context(tc.psum_pool(name="ps_acc", bufs=3))
+        ps_o = ctx.enter_context(tc.psum_pool(name="ps_o", bufs=4))
+        ps_misc = ctx.enter_context(tc.psum_pool(name="ps_misc", bufs=1))
+        ctx.enter_context(tc.manual_schedule())
+
+        mk = keep.tile([P, B, 4], BF16, name="mk")
+        nc.scalar.dma_start(out=mk[:], in_=x_mask.rearrange("b o (p e) -> p (b o) e", e=4))
+        bias = keep.tile([P, H], BF16, name="bias")
+        with nc.allow_non_contiguous_dma(reason="one bias value to a partition"):
+            nc.scalar.dma_start(out=bias[:], in_=bq.rearrange("(h a) -> a h", a=P))
+
+        wraw = {}
+        xraw = {}
+
+        def load_w(h):
+            t = keep.tile([P, DM], BF16, name="wraw%d" % h)
+            nc.sync.dma_start(out=t[:], in_=Wq[P * h : P * (h + 1), :])
+            wraw[h] = t
+
+        def load_x(b, g):
+            t = keep.tile([P, 4, T], BF16, name="xraw%d%d" % (b, g))
+            nc.sync.dma_start(out=t[:], in_=x[b, 512 * g : 512 * (g + 1), :].rearrange("(p j) t -> p j t", j=4))
+            xraw[(b, g)] = t
+
+        load_w(0)
+        load_x(0, 0)
+        load_x(0, 1)
+        load_w(1)
+        load_w(2)
+        load_w(3)
+        load_x(1, 0)
+        load_x(1, 1)
+
+        zero = keep.tile([P, 1], F32, name="zero")
+        nc.vector.memset(zero[:], 0.0)
+        warm = keep.tile([P, 1], F32, name="warm")
+        nc.scalar.activation(out=warm[:], in_=zero[:], func=ACT.Sin)
+        ones = keep.tile([P, P], BF16, name="ones")
+        nc.vector.memset(ones[:], 1.0)
+        tpos = keep.tile([P, T], F32, name="tpos")
+        nc.gpsimd.iota(tpos[:], pattern=[[1, 4], [4, 128]], base=0, channel_multiplier=0,
+                       allow_small_or_imprecise_dtypes=True)
+        ident = keep.tile([P, P], F32, name="ident")
+        make_identity(nc, ident[:])
+        swp = keep.tile([P, P], F32, name="swp")
+        nc.scalar.copy(out=swp[:, 0:64], in_=ident[:, 64:128])
+        nc.scalar.copy(out=swp[:, 64:128], in_=ident[:, 0:64])
+
+        lo = keep.tile([P, 8], F32, name="lo")
+        hi = keep.tile([P, 16], F32, name="hi")
+        nc.vector.memset(lo[:, 0:1], 1.0)
+        nc.vector.memset(hi[:, 0:1], 1.0)
+        nc.vector.tensor_scalar(out=hi[:, 0:1], in0=hi[:, 0:1], scalar1=THETA0_TURNS, scalar2=None, op0=ALU.mult)
+        for s in range(3):
+            w = 1 << s
+            nc.vector.tensor_scalar(out=lo[:, w : 2 * w], in0=lo[:, 0:w], scalar1=THETA_RATIO ** w, scalar2=None,
+                                    op0=ALU.mult)
+            nc.vector.tensor_scalar(out=hi[:, w : 2 * w], in0=hi[:, 0:w], scalar1=THETA_RATIO ** (8 * w), scalar2=None,
+                                    op0=ALU.mult)
+        nc.vector.tensor_scalar(out=hi[:, 8:16], in0=hi[:, 0:8], scalar1=-1.0, scalar2=None, op0=ALU.mult)
+        half_pi = keep.tile([P, 1], F32, name="half_pi")
+        nc.vector.tensor_scalar(out=half_pi[:], in0=lo[:, 0:1], scalar1=0.5 * math.pi, scalar2=None, op0=ALU.mult)
+        th = keep.tile([P, 16, 8], F32, name="th")
+        nc.vector.tensor_tensor(out=th[:], in0=hi[:].unsqueeze(2).to_broadcast([P, 16, 8]),
+                                in1=lo[:].unsqueeze(1).to_broadcast([P, 16, 8]), op=ALU.mult)
+
+        misc = ps_misc.tile([P, 256], F32, name="misc")
+        nc.tensor.transpose(misc[:, 0:128], th[:].rearrange("p a b -> p (a b)"), ident[:])
+        nc.tensor.matmul(misc[:, 128:136], lhsT=ones[:], rhs=mk[:].rearrange("p b e -> p (b e)"), start=True, stop=True)
+        nb = keep.tile([P, B], F32, name="nb")
+        rn = keep.tile([P, B], F32, name="rn")
+        thn = {}
+        gate = keep.tile([P, 1], F32, name="gate")
+
+        def valid_length():
+            nc.vector.tensor_reduce(out=nb[:], in_=misc[:, 128:136].rearrange("p (b e) -> p b e", e=4), axis=AX.X, op=ALU.add)
+
+        def one_over_length():
+            nc.vector.reciprocal(out=rn[:], in_=nb[:])
+
+        def turns_per_step(b):
+            t = keep.tile([P, 1], F32, name="thn%d" % b)
+            nc.vector.tensor_scalar(out=t[:], in0=rn[:, b : b + 1], scalar1=misc[:, 0:1], scalar2=None, op0=ALU.mult)
+            thn[b] = t
+
+        def open_gate():
+            nc.vector.memset(gate[:], 1.0)
+
+        tab = {}
+
+        def tab_ks(eng, b):
+            t = keep.tile([P, T], I32, name="ks%d" % b)
+            eng.tensor_scalar(out=t[:], in0=tpos[:], scalar1=thn[b][:], scalar2=0.0, op0=ALU.mult, op1=ALU.add)
+            tab[("ks", b)] = t
+
+        def tab_wc(eng, b):
+            t = keep.tile([P, T], F32, name="wc%d" % b)
+            eng.tensor_scalar(out=t[:], in0=tpos[:], scalar1=thn[b][:], scalar2=0.25, op0=ALU.mult, op1=ALU.add)
+            tab[("wc", b)] = t
+
+        def tab_kc(eng, b):
+            t = keep.tile([P, T], I32, name="kc%d" % b)
+            eng.tensor_scalar(out=t[:], in0=tpos[:], scalar1=thn[b][:], scalar2=0.25, op0=ALU.mult, op1=ALU.add)
+            tab[("kc", b)] = t
+
+        def tab_vs(b):
+            t = keep.tile([P, T], F32, name="vs%d" % b)
+            nc.vector.scalar_tensor_tensor(out=t[:], in0=tpos[:], scalar=thn[b][:], in1=tab[("ks", b)][:],
+                                           op0=ALU.mult, op1=ALU.subtract)
+            tab[("vs", b)] = t
+
+        def tab_vc(b):
+            t = keep.tile([P, T], F32, name="vc%d" % b)
+            nc.vector.tensor_tensor(out=t[:], in0=tab[("wc", b)][:], in1=tab[("kc", b)][:], op=ALU.subtract)
+            tab[("vc", b)] = t
+
+        def tab_sin(b):
+            t = keep.tile([P, T], F32, name="sin%d" % b)
+            nc.scalar.activation(out=t[:], in_=tab[("vs", b)][:], func=ACT.Sin, scale=TWO_PI)
+            tab[("sin", b)] = t
+
+        def tab_abs(b):
+            t = keep.tile([P, T], F32, name="abs%d" % b)
+            nc.scalar.activation(out=t[:], in_=tab[("vs", b)][:], func=ACT.Abs)
+            tab[("abs", b)] = t
+
+        def tab_cos(b):
+            t = keep.tile([P, T], F32, name="cos%d" % b)
+            nc.scalar.activation(out=t[:], in_=tab[("abs", b)][:], func=ACT.Sin, scale=-TWO_PI, bias=half_pi[:, 0:1])
+            tab[("cos", b)] = t
+
+        wt = {}
+        wgrp = {}
+        w_codes = {}
+        w_scales = {}
+
+        def w_transpose(h):
+            words = wraw[h][:].bitcast(F32)
+            t = ps_o.tile([P, 2, 2, P], F32, name="o")
+            for g in range(2):
+                for u in range(2):
+                    nc.tensor.transpose(t[:, g, u, :], words[:, 256 * g + u : 256 * (g + 1) : 2], ident[:])
+            wt[h] = t
+
+        def w_copy(h):
+            grp = keep.tile([P, 1024], BF16, name="wgrp%d" % h, align_bytes=64)
+            nc.scalar.copy(out=grp[:].bitcast(F32).rearrange("p (g a u) -> p g a u", g=2, u=2),
+                           in_=wt[h][:].rearrange("p g u a -> p g a u"))
+            wgrp[h] = grp
+
+        def w_quantize(h):
+            codes = keep.tile([P, 256], U32, name="wcod%d" % h, align_bytes=64)
+            scl = keep.tile([P, 256], U8, name="wscl%d" % h, align_bytes=64)
+            nc.vector.quantize_mx(out=codes[:].bitcast(FP8X4), scales=scl[:], in_=wgrp[h][:])
+            w_codes[h] = codes
+            w_scales[h] = scl
+
+        xgrp = {}
+        for b in range(B):
+            for g in range(2):
+                xgrp[(b, g)] = keep.tile([P, T, 4], BF16, name="xgrp%d%d" % (b, g), align_bytes=64)
+        x_codes = {}
+        x_scales = {}
+
+        def x_group_v(b, g, c0, c1):
+            nc.vector.tensor_copy(out=xgrp[(b, g)][:, c0:c1, :], in_=xraw[(b, g)][:, :, c0:c1].rearrange("p j t -> p t j"))
+
+        def x_group_s(b, g, c0, c1):
+            nc.scalar.copy(out=xgrp[(b, g)][:, c0:c1, :], in_=xraw[(b, g)][:, :, c0:c1].rearrange("p j t -> p t j"))
+
+        def x_group_g(b, g, c0, c1):
+            nc.gpsimd.tensor_scalar(out=xgrp[(b, g)][:, c0:c1, :], in0=xraw[(b, g)][:, :, c0:c1].rearrange("p j t -> p t j"),
+                                    scalar1=gate[:], scalar2=0.0, op0=ALU.mult, op1=ALU.add)
+
+        def x_quantize(b, g):
+            codes = keep.tile([P, T], U32, name="xcod%d%d" % (b, g), align_bytes=64)
+            scl = keep.tile([P, T], U8, name="xscl%d%d" % (b, g), align_bytes=64)
+            nc.vector.quantize_mx(out=codes[:].bitcast(FP8X4), scales=scl[:],
+                                  in_=xgrp[(b, g)][:].rearrange("p t j -> p (t j)"))
+            x_codes[(b, g)] = codes
+            x_scales[(b, g)] = scl
+
+        acc = {}
+        qs = {}
+        t1 = {}
+        t2 = {}
+        o = {}
+        res = {}
+        amax = {}
+        rcp = {}
+        fac = {}
+
+        def project(i, g):
+            b, h = divmod(i, H)
+            if g == 0:
+                acc[i] = ps_acc.tile([P, T], F32, name="acc")
+            nc.tensor.matmul_mx(
+                out=acc[i][:],
+                lhsT=w_codes[h][:, P * g : P * (g + 1)].bitcast(FP8X4),
+                lhsT_scale=w_scales[h][:, P * g : P * (g + 1)],
+                rhs=x_codes[(b, g)][:].bitcast(FP8X4),
+                rhs_scale=x_scales[(b, g)][:],
+                start=(g == 0),
+                stop=(g == 1),
+            )
+
+        def views(i):
+            b, h = divmod(i, H)
+            return (acc[i][:].rearrange("a (m t) -> a t m", t=4), bias[:, h : h + 1],
+                    tab[("cos", b)][:].rearrange("a (t m) -> a t m", t=4),
+                    tab[("sin", b)][:].rearrange("a (t m) -> a t m", t=4))
+
+        def product_cos(i):
+            accp, bcol, cview, sview = views(i)
+            t1[i] = keep.tile([P, 4, P], F32, name="t1_%d" % i)
+            nc.vector.scalar_tensor_tensor(out=t1[i][:], in0=accp, scalar=bcol, in1=cview, op0=ALU.add, op1=ALU.mult)
+
+        def product_sin(i):
+            accp, bcol, cview, sview = views(i)
+            t2[i] = keep.tile([P, 4, P], F32, name="t2_%d" % i)
+            nc.vector.scalar_tensor_tensor(out=t2[i][:], in0=accp, scalar=bcol, in1=sview, op0=ALU.add, op1=ALU.mult)
+
+        def biased_s(i):
+            accp = acc[i][:].rearrange("a (m t) -> a t m", t=4)
+            bcol = bias[:, i % H : i % H + 1]
+            qs[i] = keep.tile([P, 4, P], F32, name="qs_%d" % i)
+            nc.scalar.activation(out=qs[i][:], in_=accp, func=ACT.Identity, bias=bcol, scale=1.0)
+
+        def products_g(i):
+            accp, bcol, cview, sview = views(i)
+            t1[i] = keep.tile([P, 4, P], F32, name="t1_%d" % i)
+            t2[i] = keep.tile([P, 4, P], F32, name="t2_%d" % i)
+            nc.gpsimd.tensor_tensor(out=t1[i][:], in0=qs[i][:], in1=cview, op=ALU.mult)
+            nc.gpsimd.tensor_tensor(out=t2[i][:], in0=qs[i][:], in1=sview, op=ALU.mult)
+
+        def turn_and_add(i):
+            t = ps_o.tile([P, 4, P], F32, name="o")
+            for c in range(4):
+                nc.tensor.matmul(t[:, c, :], lhsT=t1[i][:, c, :], rhs=ident[:], is_transpose=True, start=True, stop=False)
+                nc.tensor.matmul(t[:, c, :], lhsT=t2[i][:, c, :], rhs=swp[:], is_transpose=True, start=False, stop=True)
+            o[i] = t
+
+        def empty_and_store(i):
+            b, h = divmod(i, H)
+            res[i] = keep.tile([P, 4, P], F32, name="res_%d" % i)
+            nc.scalar.copy(out=res[i][:], in_=o[i][:])
+            nc.sync.dma_start(out=out_0[h, b].rearrange("(m t) d -> m t d", t=4), in_=res[i][:])
+
+        def row_amax(i):
+            amax[i] = keep.tile([P, 4], F32, name="amax_%d" % i)
+            nc.vector.tensor_reduce(out=amax[i][:], in_=res[i][:], axis=AX.X, op=ALU.max, apply_absolute_value=True)
+
+        def row_reciprocal(i):
+            rcp[i] = keep.tile([P, 4], F32, name="rcp_%d" % i)
+            nc.vector.reciprocal(out=rcp[i][:], in_=amax[i][:])
+
+        def row_factor_s(i):
+            fac[i] = keep.tile([P, 4], F32, name="fac_%d" % i)
+            nc.scalar.activation(out=fac[i][:], in_=rcp[i][:], func=ACT.Copy, scale=448.0)
+
+        def row_factor_v(i):
+            fac[i] = keep.tile([P, 4], F32, name="fac_%d" % i)
+            nc.vector.tensor_scalar(out=fac[i][:], in0=rcp[i][:], scalar1=448.0, scalar2=None, op0=ALU.mult)
+
+        def cast_and_store(i, on_scalar):
+            b, h = divmod(i, H)
+            o8 = keep.tile([P, 4, P], FP8, name="o8_%d" % i)
+            for c in range(4):
+                if c < on_scalar:
+                    nc.scalar.activation(out=o8[:, c, :], in_=res[i][:, c, :], func=ACT.Identity,
+                                         scale=fac[i][:, c : c + 1], bias=zero[:, 0:1], saturate=False)
+                else:
+                    nc.vector.tensor_scalar(out=o8[:, c, :], in0=res[i][:, c, :], scalar1=fac[i][:, c : c + 1],
+                                            scalar2=None, op0=ALU.mult, saturate=False)
+            nc.sync.dma_start(out=out_1[h, b].rearrange("(m t) d -> m (t d)", t=4),
+                              in_=o8[:].rearrange("p t d -> p (t d)").bitcast(U8))
+
+        if True:
+            valid_length()
+            one_over_length()
+            turns_per_step(0)
+            tab_ks(nc.vector, 0)
+            w_transpose(0)
+            w_copy(0)
+            tab_vs(0)
+            x_group_s(0, 0, 352, 512)
+            tab_sin(0)
+            x_group_v(0, 0, 0, 352)
+            w_quantize(0)
+            x_group_s(0, 1, 352, 512)
+            tab_abs(0)
+            x_group_v(0, 1, 0, 352)
+            w_transpose(1)
+            w_transpose(2)
+            w_transpose(3)
+            w_copy(1)
+            w_copy(2)
+            tab_cos(0)
+            w_copy(3)
+            turns_per_step(1)
+            x_quantize(0, 0)
+            x_quantize(0, 1)
+            project(0, 0)
+            project(0, 1)
+            tab_ks(nc.vector, 1)
+            w_quantize(1)
+            w_quantize(2)
+            project(1, 0)
+            project(1, 1)
+            project(2, 0)
+            project(2, 1)
+            tab_vs(1)
+            x_group_s(1, 0, 128, 256)
+            x_group_s(1, 0, 256, 384)
+            tab_abs(1)
+            x_group_s(1, 0, 384, 512)
+            product_cos(0)
+            product_sin(0)
+            w_quantize(3)
+            turn_and_add(0)
+            empty_and_store(0)
+            project(3, 0)
+            project(3, 1)
+            product_cos(1)
+            product_sin(1)
+            turn_and_add(1)
+            x_group_s(1, 1, 128, 256)
+            empty_and_store(1)
+            product_cos(2)
+            row_amax(0)
+            product_sin(2)
+            row_reciprocal(0)
+            turn_and_add(2)
+            x_group_s(1, 1, 256, 384)
+            tab_sin(1)
+            tab_cos(1)
+            empty_and_store(2)
+            row_factor_s(0)
+            product_cos(3)
+            row_amax(1)
+            product_sin(3)
+            row_reciprocal(1)
+            turn_and_add(3)
+            x_group_s(1, 1, 384, 512)
+            empty_and_store(3)
+            row_factor_s(1)
+            x_group_v(1, 0, 0, 128)
+            x_group_v(1, 1, 0, 128)
+            x_quantize(1, 0)
+            project(4, 0)
+            project(5, 0)
+            project(6, 0)
+            x_quantize(1, 1)
+            project(4, 1)
+            project(5, 1)
+            project(6, 1)
+            cast_and_store(0, 4)
+            cast_and_store(1, 4)
+            row_amax(2)
+            row_amax(3)
+            row_reciprocal(2)
+            row_factor_s(2)
+            product_cos(4)
+            row_reciprocal(3)
+            row_factor_s(3)
+            product_sin(4)
+            project(7, 0)
+            project(7, 1)
+            cast_and_store(2, 4)
+            product_cos(5)
+            product_sin(5)
+            turn_and_add(4)
+            cast_and_store(3, 4)
+            product_cos(6)
+            product_sin(6)
+            turn_and_add(5)
+            empty_and_store(4)
+            product_cos(7)
+            product_sin(7)
+            turn_and_add(6)
+            empty_and_store(5)
+            turn_and_add(7)
+            empty_and_store(6)
+            row_amax(4)
+            empty_and_store(7)
+            row_amax(5)
+            row_reciprocal(4)
+            row_factor_s(4)
+            row_amax(6)
+            row_reciprocal(5)
+            row_factor_s(5)
+            row_amax(7)
+            cast_and_store(4, 4)
+            row_reciprocal(6)
+            row_reciprocal(7)
+            row_factor_v(6)
+            row_factor_v(7)
+            cast_and_store(6, 0)
+            cast_and_store(5, 4)
+            cast_and_store(7, 0)

@@ -193,10 +193,12 @@ def tile_attentionmodule_pa_kernel(tc, x, x_mask, Wq, bq, out_0, out_1):
         x_scales = {}
 
         def x_group_v(b, g, c0, c1):
-            nc.vector.tensor_copy(out=xgrp[(b, g)][:, c0:c1, :], in_=xraw[(b, g)][:, :, c0:c1].rearrange("p j t -> p t j"))
+            nc.vector.tensor_copy(out=xgrp[(b, g)][:, c0:c1, :].rearrange("p (c i) j -> p c j i", i=4),
+                                  in_=xraw[(b, g)][:, :, c0:c1].rearrange("p j (c i) -> p c j i", i=4))
 
         def x_group_s(b, g, c0, c1):
-            nc.scalar.copy(out=xgrp[(b, g)][:, c0:c1, :], in_=xraw[(b, g)][:, :, c0:c1].rearrange("p j t -> p t j"))
+            nc.scalar.copy(out=xgrp[(b, g)][:, c0:c1, :].rearrange("p (c i) j -> p c j i", i=4),
+                           in_=xraw[(b, g)][:, :, c0:c1].rearrange("p j (c i) -> p c j i", i=4))
 
         def x_group_g(b, g, c0, c1):
             nc.gpsimd.tensor_scalar(out=xgrp[(b, g)][:, c0:c1, :], in0=xraw[(b, g)][:, :, c0:c1].rearrange("p j t -> p t j"),

@@ -19,6 +19,7 @@ ACT = mybir.ActivationFunctionType
 AX = mybir.AxisListType
 
 P = 128
+TILES = B * H
 TWO_PI = 2.0 * math.pi
 THETA0_TURNS = 10.0 / TWO_PI
 THETA_RATIO = 10000.0 ** (-2.0 / HD)
@@ -67,11 +68,11 @@ def tile_attentionmodule_pa_kernel(tc, x, x_mask, Wq, bq, out_0, out_1):
         nc.scalar.activation(out=warm[:], in_=zero[:], func=ACT.Sin)
         ones = keep.tile([P, P], BF16, name="ones")
         nc.vector.memset(ones[:], 1.0)
+        ident = keep.tile([P, P], F32, name="ident")
+        make_identity(nc, ident[:])
         tpos = keep.tile([P, T], F32, name="tpos")
         nc.gpsimd.iota(tpos[:], pattern=[[1, 4], [4, 128]], base=0, channel_multiplier=0,
                        allow_small_or_imprecise_dtypes=True)
-        ident = keep.tile([P, P], F32, name="ident")
-        make_identity(nc, ident[:])
         swp = keep.tile([P, P], F32, name="swp")
         nc.scalar.copy(out=swp[:, 0:64], in_=ident[:, 64:128])
         nc.scalar.copy(out=swp[:, 64:128], in_=ident[:, 0:64])
@@ -95,8 +96,8 @@ def tile_attentionmodule_pa_kernel(tc, x, x_mask, Wq, bq, out_0, out_1):
                                 in1=lo[:].unsqueeze(1).to_broadcast([P, 16, 8]), op=ALU.mult)
 
         misc = ps_misc.tile([P, 256], F32, name="misc")
-        nc.tensor.transpose(misc[:, 0:128], th[:].rearrange("p a b -> p (a b)"), ident[:])
         nc.tensor.matmul(misc[:, 128:136], lhsT=ones[:], rhs=mk[:].rearrange("p b e -> p (b e)"), start=True, stop=True)
+        nc.tensor.transpose(misc[:, 0:128], th[:].rearrange("p a b -> p (a b)"), ident[:])
         nb = keep.tile([P, B], F32, name="nb")
         rn = keep.tile([P, B], F32, name="rn")
         thn = {}
@@ -118,31 +119,16 @@ def tile_attentionmodule_pa_kernel(tc, x, x_mask, Wq, bq, out_0, out_1):
 
         tab = {}
 
-        def tab_ks(eng, b):
+        def tab_ks(b):
             t = keep.tile([P, T], I32, name="ks%d" % b)
-            eng.tensor_scalar(out=t[:], in0=tpos[:], scalar1=thn[b][:], scalar2=0.0, op0=ALU.mult, op1=ALU.add)
+            nc.vector.tensor_scalar(out=t[:], in0=tpos[:], scalar1=thn[b][:], scalar2=0.0, op0=ALU.mult, op1=ALU.add)
             tab[("ks", b)] = t
-
-        def tab_wc(eng, b):
-            t = keep.tile([P, T], F32, name="wc%d" % b)
-            eng.tensor_scalar(out=t[:], in0=tpos[:], scalar1=thn[b][:], scalar2=0.25, op0=ALU.mult, op1=ALU.add)
-            tab[("wc", b)] = t
-
-        def tab_kc(eng, b):
-            t = keep.tile([P, T], I32, name="kc%d" % b)
-            eng.tensor_scalar(out=t[:], in0=tpos[:], scalar1=thn[b][:], scalar2=0.25, op0=ALU.mult, op1=ALU.add)
-            tab[("kc", b)] = t
 
         def tab_vs(b):
             t = keep.tile([P, T], F32, name="vs%d" % b)
             nc.vector.scalar_tensor_tensor(out=t[:], in0=tpos[:], scalar=thn[b][:], in1=tab[("ks", b)][:],
                                            op0=ALU.mult, op1=ALU.subtract)
             tab[("vs", b)] = t
-
-        def tab_vc(b):
-            t = keep.tile([P, T], F32, name="vc%d" % b)
-            nc.vector.tensor_tensor(out=t[:], in0=tab[("wc", b)][:], in1=tab[("kc", b)][:], op=ALU.subtract)
-            tab[("vc", b)] = t
 
         def tab_sin(b):
             t = keep.tile([P, T], F32, name="sin%d" % b)
@@ -213,57 +199,44 @@ def tile_attentionmodule_pa_kernel(tc, x, x_mask, Wq, bq, out_0, out_1):
             x_scales[(b, g)] = scl
 
         acc = {}
-        qs = {}
         t1 = {}
         t2 = {}
         o = {}
         res = {}
-        amax = {}
-        rcp = {}
+        amax = keep.tile([P, TILES, 4], F32, name="amax")
+        rcp = keep.tile([P, TILES, 4], F32, name="rcp")
         fac = {}
+        for e in ("g", "s", "v"):
+            fac[e] = keep.tile([P, TILES, 4], F32, name="fac_" + e)
+        fac_of = {}
 
-        def project(i, g):
+        def project(i):
             b, h = divmod(i, H)
-            if g == 0:
-                acc[i] = ps_acc.tile([P, T], F32, name="acc")
-            nc.tensor.matmul_mx(
-                out=acc[i][:],
-                lhsT=w_codes[h][:, P * g : P * (g + 1)].bitcast(FP8X4),
-                lhsT_scale=w_scales[h][:, P * g : P * (g + 1)],
-                rhs=x_codes[(b, g)][:].bitcast(FP8X4),
-                rhs_scale=x_scales[(b, g)][:],
-                start=(g == 0),
-                stop=(g == 1),
-            )
+            acc[i] = ps_acc.tile([P, T], F32, name="acc")
+            for g in range(2):
+                nc.tensor.matmul_mx(
+                    out=acc[i][:],
+                    lhsT=w_codes[h][:, P * g : P * (g + 1)].bitcast(FP8X4),
+                    lhsT_scale=w_scales[h][:, P * g : P * (g + 1)],
+                    rhs=x_codes[(b, g)][:].bitcast(FP8X4),
+                    rhs_scale=x_scales[(b, g)][:],
+                    start=(g == 0),
+                    stop=(g == 1),
+                )
 
-        def views(i):
+        def product(i, which, dest):
             b, h = divmod(i, H)
-            return (acc[i][:].rearrange("a (m t) -> a t m", t=4), bias[:, h : h + 1],
-                    tab[("cos", b)][:].rearrange("a (t m) -> a t m", t=4),
-                    tab[("sin", b)][:].rearrange("a (t m) -> a t m", t=4))
+            dest[i] = keep.tile([P, 4, P], F32, name="%s_%d" % (which, i))
+            nc.vector.scalar_tensor_tensor(out=dest[i][:], in0=acc[i][:].rearrange("a (m t) -> a t m", t=4),
+                                           scalar=bias[:, h : h + 1],
+                                           in1=tab[(which, b)][:].rearrange("a (t m) -> a t m", t=4),
+                                           op0=ALU.add, op1=ALU.mult)
 
         def product_cos(i):
-            accp, bcol, cview, sview = views(i)
-            t1[i] = keep.tile([P, 4, P], F32, name="t1_%d" % i)
-            nc.vector.scalar_tensor_tensor(out=t1[i][:], in0=accp, scalar=bcol, in1=cview, op0=ALU.add, op1=ALU.mult)
+            product(i, "cos", t1)
 
         def product_sin(i):
-            accp, bcol, cview, sview = views(i)
-            t2[i] = keep.tile([P, 4, P], F32, name="t2_%d" % i)
-            nc.vector.scalar_tensor_tensor(out=t2[i][:], in0=accp, scalar=bcol, in1=sview, op0=ALU.add, op1=ALU.mult)
-
-        def biased_s(i):
-            accp = acc[i][:].rearrange("a (m t) -> a t m", t=4)
-            bcol = bias[:, i % H : i % H + 1]
-            qs[i] = keep.tile([P, 4, P], F32, name="qs_%d" % i)
-            nc.scalar.activation(out=qs[i][:], in_=accp, func=ACT.Identity, bias=bcol, scale=1.0)
-
-        def products_g(i):
-            accp, bcol, cview, sview = views(i)
-            t1[i] = keep.tile([P, 4, P], F32, name="t1_%d" % i)
-            t2[i] = keep.tile([P, 4, P], F32, name="t2_%d" % i)
-            nc.gpsimd.tensor_tensor(out=t1[i][:], in0=qs[i][:], in1=cview, op=ALU.mult)
-            nc.gpsimd.tensor_tensor(out=t2[i][:], in0=qs[i][:], in1=sview, op=ALU.mult)
+            product(i, "sin", t2)
 
         def turn_and_add(i):
             t = ps_o.tile([P, 4, P], F32, name="o")
@@ -279,154 +252,169 @@ def tile_attentionmodule_pa_kernel(tc, x, x_mask, Wq, bq, out_0, out_1):
             nc.sync.dma_start(out=out_0[h, b].rearrange("(m t) d -> m t d", t=4), in_=res[i][:])
 
         def row_amax(i):
-            amax[i] = keep.tile([P, 4], F32, name="amax_%d" % i)
-            nc.vector.tensor_reduce(out=amax[i][:], in_=res[i][:], axis=AX.X, op=ALU.max, apply_absolute_value=True)
+            nc.vector.tensor_reduce(out=amax[:, i, :], in_=res[i][:], axis=AX.X, op=ALU.max, apply_absolute_value=True)
 
-        def row_reciprocal(i):
-            rcp[i] = keep.tile([P, 4], F32, name="rcp_%d" % i)
-            nc.vector.reciprocal(out=rcp[i][:], in_=amax[i][:])
+        def row_reciprocal(i0, i1):
+            nc.vector.reciprocal(out=rcp[:, i0:i1, :].rearrange("p i c -> p (i c)"),
+                                 in_=amax[:, i0:i1, :].rearrange("p i c -> p (i c)"))
 
-        def row_factor_s(i):
-            fac[i] = keep.tile([P, 4], F32, name="fac_%d" % i)
-            nc.scalar.activation(out=fac[i][:], in_=rcp[i][:], func=ACT.Copy, scale=448.0)
+        def row_factor(e, i0, i1):
+            dst = fac[e][:, i0:i1, :].rearrange("p i c -> p (i c)")
+            src = rcp[:, i0:i1, :].rearrange("p i c -> p (i c)")
+            if e == "g":
+                nc.gpsimd.tensor_scalar(out=dst, in0=src, scalar1=448.0, scalar2=0.0, op0=ALU.mult, op1=ALU.add)
+            elif e == "s":
+                nc.scalar.activation(out=dst, in_=src, func=ACT.Copy, scale=448.0)
+            else:
+                nc.vector.tensor_scalar(out=dst, in0=src, scalar1=448.0, scalar2=None, op0=ALU.mult)
+            for i in range(i0, i1):
+                fac_of[i] = fac[e]
 
-        def row_factor_v(i):
-            fac[i] = keep.tile([P, 4], F32, name="fac_%d" % i)
-            nc.vector.tensor_scalar(out=fac[i][:], in0=rcp[i][:], scalar1=448.0, scalar2=None, op0=ALU.mult)
+        o8 = {}
 
-        def cast_and_store(i, on_scalar):
-            b, h = divmod(i, H)
-            o8 = keep.tile([P, 4, P], FP8, name="o8_%d" % i)
+        def bytes_tile(i):
+            if i not in o8:
+                o8[i] = keep.tile([P, 4, P], FP8, name="o8_%d" % i)
+            return o8[i]
+
+        def cast_s(i, c0=0, c1=4):
+            for c in range(c0, c1):
+                nc.scalar.activation(out=bytes_tile(i)[:, c, :], in_=res[i][:, c, :], func=ACT.Identity,
+                                     scale=fac_of[i][:, i, c : c + 1], bias=zero[:, 0:1], saturate=False)
+
+        def cast_v(i, c0=0, c1=4):
+            for c in range(c0, c1):
+                nc.vector.tensor_scalar(out=bytes_tile(i)[:, c, :], in0=res[i][:, c, :], scalar1=fac_of[i][:, i, c : c + 1],
+                                        scalar2=None, op0=ALU.mult, saturate=False)
+
+        def cast_g(i):
+            scaled = keep.tile([P, 4, P], F32, name="scaled_%d" % i)
             for c in range(4):
-                if c < on_scalar:
-                    nc.scalar.activation(out=o8[:, c, :], in_=res[i][:, c, :], func=ACT.Identity,
-                                         scale=fac[i][:, c : c + 1], bias=zero[:, 0:1], saturate=False)
-                else:
-                    nc.vector.tensor_scalar(out=o8[:, c, :], in0=res[i][:, c, :], scalar1=fac[i][:, c : c + 1],
-                                            scalar2=None, op0=ALU.mult, saturate=False)
-            nc.sync.dma_start(out=out_1[h, b].rearrange("(m t) d -> m (t d)", t=4),
-                              in_=o8[:].rearrange("p t d -> p (t d)").bitcast(U8))
+                nc.gpsimd.tensor_scalar(out=scaled[:, c, :], in0=res[i][:, c, :], scalar1=fac_of[i][:, i, c : c + 1],
+                                        scalar2=0.0, op0=ALU.mult, op1=ALU.add)
+            nc.gpsimd.tensor_copy(out=bytes_tile(i)[:].rearrange("p t d -> p (t d)"),
+                                  in_=scaled[:].rearrange("p t d -> p (t d)"), saturate=False)
 
-        if True:
-            valid_length()
-            one_over_length()
-            turns_per_step(0)
-            tab_ks(nc.vector, 0)
-            w_transpose(0)
-            w_copy(0)
-            tab_vs(0)
-            x_group_s(0, 0, 352, 512)
-            tab_sin(0)
-            x_group_v(0, 0, 0, 352)
-            w_quantize(0)
-            x_group_s(0, 1, 352, 512)
-            tab_abs(0)
-            x_group_v(0, 1, 0, 352)
-            w_transpose(1)
-            w_transpose(2)
-            w_transpose(3)
-            w_copy(1)
-            w_copy(2)
-            tab_cos(0)
-            w_copy(3)
-            turns_per_step(1)
-            x_quantize(0, 0)
-            x_quantize(0, 1)
-            project(0, 0)
-            project(0, 1)
-            tab_ks(nc.vector, 1)
-            w_quantize(1)
-            w_quantize(2)
-            project(1, 0)
-            project(1, 1)
-            project(2, 0)
-            project(2, 1)
-            tab_vs(1)
-            x_group_s(1, 0, 128, 256)
-            x_group_s(1, 0, 256, 384)
-            tab_abs(1)
-            x_group_s(1, 0, 384, 512)
-            product_cos(0)
-            product_sin(0)
-            w_quantize(3)
-            turn_and_add(0)
-            empty_and_store(0)
-            project(3, 0)
-            project(3, 1)
-            product_cos(1)
-            product_sin(1)
-            turn_and_add(1)
-            x_group_s(1, 1, 128, 256)
-            empty_and_store(1)
-            product_cos(2)
-            row_amax(0)
-            product_sin(2)
-            row_reciprocal(0)
-            turn_and_add(2)
-            x_group_s(1, 1, 256, 384)
-            tab_sin(1)
-            tab_cos(1)
-            empty_and_store(2)
-            row_factor_s(0)
-            product_cos(3)
-            row_amax(1)
-            product_sin(3)
-            row_reciprocal(1)
-            turn_and_add(3)
-            x_group_s(1, 1, 384, 512)
-            empty_and_store(3)
-            row_factor_s(1)
-            x_group_v(1, 0, 0, 128)
-            x_group_v(1, 1, 0, 128)
-            x_quantize(1, 0)
-            project(4, 0)
-            project(5, 0)
-            project(6, 0)
-            x_quantize(1, 1)
-            project(4, 1)
-            project(5, 1)
-            project(6, 1)
-            cast_and_store(0, 4)
-            cast_and_store(1, 4)
-            row_amax(2)
-            row_amax(3)
-            row_reciprocal(2)
-            row_factor_s(2)
-            product_cos(4)
-            row_reciprocal(3)
-            row_factor_s(3)
-            product_sin(4)
-            project(7, 0)
-            project(7, 1)
-            cast_and_store(2, 4)
-            product_cos(5)
-            product_sin(5)
-            turn_and_add(4)
-            cast_and_store(3, 4)
-            product_cos(6)
-            product_sin(6)
-            turn_and_add(5)
-            empty_and_store(4)
-            product_cos(7)
-            product_sin(7)
-            turn_and_add(6)
-            empty_and_store(5)
-            turn_and_add(7)
-            empty_and_store(6)
-            row_amax(4)
-            empty_and_store(7)
-            row_amax(5)
-            row_reciprocal(4)
-            row_factor_s(4)
-            row_amax(6)
-            row_reciprocal(5)
-            row_factor_s(5)
-            row_amax(7)
-            cast_and_store(4, 4)
-            row_reciprocal(6)
-            row_reciprocal(7)
-            row_factor_v(6)
-            row_factor_v(7)
-            cast_and_store(6, 0)
-            cast_and_store(5, 4)
-            cast_and_store(7, 0)
+        def store_bytes(i):
+            b, h = divmod(i, H)
+            nc.sync.dma_start(out=out_1[h, b].rearrange("(m t) d -> m (t d)", t=4),
+                              in_=o8[i][:].rearrange("p t d -> p (t d)").bitcast(U8))
+
+        valid_length()
+        one_over_length()
+        turns_per_step(0)
+        turns_per_step(1)
+        tab_ks(0)
+        tab_ks(1)
+        w_transpose(0)
+        w_copy(0)
+        tab_vs(0)
+        x_group_s(0, 0, 352, 512)
+        tab_sin(0)
+        x_group_v(0, 0, 0, 352)
+        w_quantize(0)
+        x_group_s(0, 1, 352, 512)
+        tab_abs(0)
+        x_group_v(0, 1, 0, 352)
+        w_transpose(1)
+        w_transpose(2)
+        w_transpose(3)
+        w_copy(1)
+        w_copy(2)
+        tab_cos(0)
+        w_copy(3)
+        x_quantize(0, 0)
+        x_quantize(0, 1)
+        project(0)
+        tab_vs(1)
+        w_quantize(1)
+        w_quantize(2)
+        project(1)
+        project(2)
+        x_group_s(1, 0, 256, 384)
+        x_group_s(1, 0, 384, 512)
+        x_group_s(1, 1, 256, 384)
+        x_group_s(1, 1, 384, 512)
+
+        product_cos(0)
+        product_sin(0)
+        w_quantize(3)
+        open_gate()
+        x_group_g(1, 0, 0, 256)
+        x_group_g(1, 1, 0, 256)
+        turn_and_add(0)
+        empty_and_store(0)
+        project(3)
+        tab_abs(1)
+        product_cos(1)
+        product_sin(1)
+        turn_and_add(1)
+        empty_and_store(1)
+        tab_sin(1)
+        tab_cos(1)
+        product_cos(2)
+        product_sin(2)
+        turn_and_add(2)
+        empty_and_store(2)
+        product_cos(3)
+        product_sin(3)
+        turn_and_add(3)
+        empty_and_store(3)
+        x_quantize(1, 0)
+        x_quantize(1, 1)
+        project(4)
+        project(5)
+        row_amax(0)
+        row_amax(1)
+        product_cos(4)
+        row_reciprocal(0, 2)
+        row_factor("g", 0, 2)
+        product_sin(4)
+        turn_and_add(4)
+        project(6)
+        project(7)
+        cast_s(0)
+        store_bytes(0)
+        row_amax(2)
+        cast_s(1)
+        store_bytes(1)
+        empty_and_store(4)
+        product_cos(5)
+        row_reciprocal(2, 3)
+        row_factor("g", 2, 3)
+        product_sin(5)
+        turn_and_add(5)
+        row_amax(3)
+        cast_s(2)
+        store_bytes(2)
+        empty_and_store(5)
+        product_cos(6)
+        row_reciprocal(3, 4)
+        row_factor("g", 3, 4)
+        product_sin(6)
+        turn_and_add(6)
+        cast_s(3)
+        store_bytes(3)
+        empty_and_store(6)
+        product_cos(7)
+        product_sin(7)
+        turn_and_add(7)
+        row_amax(4)
+        row_amax(5)
+        row_reciprocal(4, 5)
+        row_factor("g", 4, 5)
+        cast_g(4)
+        empty_and_store(7)
+        row_amax(6)
+        row_reciprocal(5, 7)
+        row_factor("s", 5, 7)
+        cast_s(5)
+        store_bytes(5)
+        row_amax(7)
+        cast_s(6)
+        store_bytes(6)
+        store_bytes(4)
+        row_reciprocal(7, 8)
+        row_factor("v", 7, 8)
+        cast_v(7)
+        store_bytes(7)

@@ -287,14 +287,6 @@ def tile_attentionmodule_pa_kernel(tc, x, x_mask, Wq, bq, out_0, out_1):
                 nc.vector.tensor_scalar(out=bytes_tile(i)[:, c, :], in0=res[i][:, c, :], scalar1=fac_of[i][:, i, c : c + 1],
                                         scalar2=None, op0=ALU.mult, saturate=False)
 
-        def cast_g(i):
-            scaled = keep.tile([P, 4, P], F32, name="scaled_%d" % i)
-            for c in range(4):
-                nc.gpsimd.tensor_scalar(out=scaled[:, c, :], in0=res[i][:, c, :], scalar1=fac_of[i][:, i, c : c + 1],
-                                        scalar2=0.0, op0=ALU.mult, op1=ALU.add)
-            nc.gpsimd.tensor_copy(out=bytes_tile(i)[:].rearrange("p t d -> p (t d)"),
-                                  in_=scaled[:].rearrange("p t d -> p (t d)"), saturate=False)
-
         def store_bytes(i):
             b, h = divmod(i, H)
             nc.sync.dma_start(out=out_1[h, b].rearrange("(m t) d -> m (t d)", t=4),
@@ -403,18 +395,20 @@ def tile_attentionmodule_pa_kernel(tc, x, x_mask, Wq, bq, out_0, out_1):
         row_amax(5)
         row_reciprocal(4, 5)
         row_factor("g", 4, 5)
-        cast_g(4)
         empty_and_store(7)
         row_amax(6)
         row_reciprocal(5, 7)
-        row_factor("s", 5, 7)
+        row_factor("g", 5, 7)
+        cast_s(4)
+        store_bytes(4)
+        row_amax(7)
+        cast_v(6, 0, 2)
         cast_s(5)
         store_bytes(5)
-        row_amax(7)
-        cast_s(6)
-        store_bytes(6)
-        store_bytes(4)
         row_reciprocal(7, 8)
+        cast_v(6, 2, 4)
+        store_bytes(6)
         row_factor("v", 7, 8)
-        cast_v(7)
+        cast_v(7, 0, 2)
+        cast_s(7, 2, 4)
         store_bytes(7)

@@ -76,6 +76,8 @@ def tile_attentionmodule_pa_kernel(tc, x, x_mask, Wq, bq, out_0, out_1):
         swp = keep.tile([P, P], F32, name="swp")
         nc.scalar.copy(out=swp[:, 0:64], in_=ident[:, 64:128])
         nc.scalar.copy(out=swp[:, 64:128], in_=ident[:, 0:64])
+        wide = keep.tile([P, T], BF16, name="wide")
+        nc.scalar.copy(out=wide[:], in_=ones[:, 0:1].to_broadcast([P, T]))
 
         lo = keep.tile([P, 8], F32, name="lo")
         hi = keep.tile([P, 16], F32, name="hi")
@@ -95,6 +97,13 @@ def tile_attentionmodule_pa_kernel(tc, x, x_mask, Wq, bq, out_0, out_1):
         nc.vector.tensor_tensor(out=th[:], in0=hi[:].unsqueeze(2).to_broadcast([P, 16, 8]),
                                 in1=lo[:].unsqueeze(1).to_broadcast([P, 16, 8]), op=ALU.mult)
 
+        idle_sums = ps_acc.tile([P, T], F32, name="acc")
+
+        def raise_clock(passes, moving, width):
+            for k in range(passes):
+                nc.tensor.matmul(idle_sums[:, 0:width], lhsT=ones[:], rhs=moving, start=True, stop=True)
+
+        raise_clock(8, ones[:], P)
         misc = ps_misc.tile([P, 256], F32, name="misc")
         nc.tensor.matmul(misc[:, 128:136], lhsT=ones[:], rhs=mk[:].rearrange("p b e -> p (b e)"), start=True, stop=True)
         nc.tensor.transpose(misc[:, 0:128], th[:].rearrange("p a b -> p (a b)"), ident[:])
@@ -299,6 +308,7 @@ def tile_attentionmodule_pa_kernel(tc, x, x_mask, Wq, bq, out_0, out_1):
         tab_ks(0)
         tab_ks(1)
         w_transpose(0)
+        raise_clock(4, wide[:], T)
         w_copy(0)
         tab_vs(0)
         x_group_s(0, 0, 352, 512)

@@ -105,23 +105,18 @@ def tile_attentionmodule_pa_kernel(tc, x, x_mask, Wq, bq, out_0, out_1):
 
         raise_clock(8, ones[:], P)
         misc = ps_misc.tile([P, 256], F32, name="misc")
-        nc.tensor.matmul(misc[:, 128:136], lhsT=ones[:], rhs=mk[:].rearrange("p b e -> p (b e)"), start=True, stop=True)
         nc.tensor.transpose(misc[:, 0:128], th[:].rearrange("p a b -> p (a b)"), ident[:])
-        nb = keep.tile([P, B], F32, name="nb")
+        for e in range(4):
+            nc.tensor.matmul(misc[:, 128:130], lhsT=ones[:], rhs=mk[:, :, e], start=(e == 0), stop=(e == 3))
         rn = keep.tile([P, B], F32, name="rn")
-        thn = {}
         gate = keep.tile([P, 1], F32, name="gate")
+        tth = keep.tile([P, T], F32, name="tth")
 
-        def valid_length():
-            nc.vector.tensor_reduce(out=nb[:], in_=misc[:, 128:136].rearrange("p (b e) -> p b e", e=4), axis=AX.X, op=ALU.add)
+        def token_times_theta():
+            nc.vector.tensor_scalar(out=tth[:], in0=tpos[:], scalar1=misc[:, 0:1], scalar2=None, op0=ALU.mult)
 
         def one_over_length():
-            nc.vector.reciprocal(out=rn[:], in_=nb[:])
-
-        def turns_per_step(b):
-            t = keep.tile([P, 1], F32, name="thn%d" % b)
-            nc.vector.tensor_scalar(out=t[:], in0=rn[:, b : b + 1], scalar1=misc[:, 0:1], scalar2=None, op0=ALU.mult)
-            thn[b] = t
+            nc.vector.reciprocal(out=rn[:], in_=misc[:, 128:130])
 
         def open_gate():
             nc.vector.memset(gate[:], 1.0)
@@ -130,12 +125,12 @@ def tile_attentionmodule_pa_kernel(tc, x, x_mask, Wq, bq, out_0, out_1):
 
         def tab_ks(b):
             t = keep.tile([P, T], I32, name="ks%d" % b)
-            nc.vector.tensor_scalar(out=t[:], in0=tpos[:], scalar1=thn[b][:], scalar2=0.0, op0=ALU.mult, op1=ALU.add)
+            nc.vector.tensor_scalar(out=t[:], in0=tth[:], scalar1=rn[:, b : b + 1], scalar2=0.0, op0=ALU.mult, op1=ALU.add)
             tab[("ks", b)] = t
 
         def tab_vs(b):
             t = keep.tile([P, T], F32, name="vs%d" % b)
-            nc.vector.scalar_tensor_tensor(out=t[:], in0=tpos[:], scalar=thn[b][:], in1=tab[("ks", b)][:],
+            nc.vector.scalar_tensor_tensor(out=t[:], in0=tth[:], scalar=rn[:, b : b + 1], in1=tab[("ks", b)][:],
                                            op0=ALU.mult, op1=ALU.subtract)
             tab[("vs", b)] = t
 
@@ -301,10 +296,8 @@ def tile_attentionmodule_pa_kernel(tc, x, x_mask, Wq, bq, out_0, out_1):
             nc.sync.dma_start(out=out_1[h, b].rearrange("(m t) d -> m (t d)", t=4),
                               in_=o8[i][:].rearrange("p t d -> p (t d)").bitcast(U8))
 
-        valid_length()
+        token_times_theta()
         one_over_length()
-        turns_per_step(0)
-        turns_per_step(1)
         tab_ks(0)
         tab_ks(1)
         w_transpose(0)

@@ -67,7 +67,6 @@ def tile_attentionmodule_pa_kernel(tc, x, x_mask, Wq, bq, out_0, out_1):
         warm = keep.tile([P, 1], F32, name="warm")
         nc.scalar.activation(out=warm[:], in_=zero[:], func=ACT.Sin)
         ones = keep.tile([P, P], BF16, name="ones")
-        nc.vector.memset(ones[:], 1.0)
         ident = keep.tile([P, P], F32, name="ident")
         make_identity(nc, ident[:])
         tpos = keep.tile([P, T], F32, name="tpos")
@@ -76,26 +75,23 @@ def tile_attentionmodule_pa_kernel(tc, x, x_mask, Wq, bq, out_0, out_1):
         swp = keep.tile([P, P], F32, name="swp")
         nc.scalar.copy(out=swp[:, 0:64], in_=ident[:, 64:128])
         nc.scalar.copy(out=swp[:, 64:128], in_=ident[:, 0:64])
+
+        unit = keep.tile([P, 64], F32, name="unit")
+        nc.vector.memset(unit[:], 1.0)
+        none = keep.tile([P, 64], F32, name="none")
+        nc.vector.memset(none[:], 0.0)
+        ratio = keep.tile([P, 64], F32, name="ratio")
+        nc.vector.tensor_scalar(out=ratio[:], in0=unit[:], scalar1=THETA_RATIO, scalar2=None, op0=ALU.mult)
+        th = keep.tile([P, P], F32, name="th")
+        nc.vector.tensor_tensor_scan(out=th[:, 0:64], data0=ratio[:], data1=none[:], initial=THETA0_TURNS / THETA_RATIO,
+                                     op0=ALU.mult, op1=ALU.add)
+        nc.vector.tensor_tensor_scan(out=th[:, 64:128], data0=ratio[:], data1=none[:], initial=-THETA0_TURNS / THETA_RATIO,
+                                     op0=ALU.mult, op1=ALU.add)
+        nc.vector.memset(ones[:], 1.0)
         wide = keep.tile([P, T], BF16, name="wide")
         nc.scalar.copy(out=wide[:], in_=ones[:, 0:1].to_broadcast([P, T]))
-
-        lo = keep.tile([P, 8], F32, name="lo")
-        hi = keep.tile([P, 16], F32, name="hi")
-        nc.vector.memset(lo[:, 0:1], 1.0)
-        nc.vector.memset(hi[:, 0:1], 1.0)
-        nc.vector.tensor_scalar(out=hi[:, 0:1], in0=hi[:, 0:1], scalar1=THETA0_TURNS, scalar2=None, op0=ALU.mult)
-        for s in range(3):
-            w = 1 << s
-            nc.vector.tensor_scalar(out=lo[:, w : 2 * w], in0=lo[:, 0:w], scalar1=THETA_RATIO ** w, scalar2=None,
-                                    op0=ALU.mult)
-            nc.vector.tensor_scalar(out=hi[:, w : 2 * w], in0=hi[:, 0:w], scalar1=THETA_RATIO ** (8 * w), scalar2=None,
-                                    op0=ALU.mult)
-        nc.vector.tensor_scalar(out=hi[:, 8:16], in0=hi[:, 0:8], scalar1=-1.0, scalar2=None, op0=ALU.mult)
         half_pi = keep.tile([P, 1], F32, name="half_pi")
-        nc.vector.tensor_scalar(out=half_pi[:], in0=lo[:, 0:1], scalar1=0.5 * math.pi, scalar2=None, op0=ALU.mult)
-        th = keep.tile([P, 16, 8], F32, name="th")
-        nc.vector.tensor_tensor(out=th[:], in0=hi[:].unsqueeze(2).to_broadcast([P, 16, 8]),
-                                in1=lo[:].unsqueeze(1).to_broadcast([P, 16, 8]), op=ALU.mult)
+        nc.vector.tensor_scalar(out=half_pi[:], in0=unit[:, 0:1], scalar1=0.5 * math.pi, scalar2=None, op0=ALU.mult)
 
         idle_sums = ps_acc.tile([P, T], F32, name="acc")
 
@@ -103,9 +99,9 @@ def tile_attentionmodule_pa_kernel(tc, x, x_mask, Wq, bq, out_0, out_1):
             for k in range(passes):
                 nc.tensor.matmul(idle_sums[:, 0:width], lhsT=ones[:], rhs=moving, start=True, stop=True)
 
-        raise_clock(8, ones[:], P)
         misc = ps_misc.tile([P, 256], F32, name="misc")
-        nc.tensor.transpose(misc[:, 0:128], th[:].rearrange("p a b -> p (a b)"), ident[:])
+        nc.tensor.transpose(misc[:, 0:128], th[:], ident[:])
+        raise_clock(8, ones[:], P)
         for e in range(4):
             nc.tensor.matmul(misc[:, 128:130], lhsT=ones[:], rhs=mk[:, :, e], start=(e == 0), stop=(e == 3))
         rn = keep.tile([P, B], F32, name="rn")
@@ -228,35 +224,53 @@ def tile_attentionmodule_pa_kernel(tc, x, x_mask, Wq, bq, out_0, out_1):
                     stop=(g == 1),
                 )
 
-        def product(i, which, dest):
-            b, h = divmod(i, H)
-            dest[i] = keep.tile([P, 4, P], F32, name="%s_%d" % (which, i))
-            nc.vector.scalar_tensor_tensor(out=dest[i][:], in0=acc[i][:].rearrange("a (m t) -> a t m", t=4),
-                                           scalar=bias[:, h : h + 1],
-                                           in1=tab[(which, b)][:].rearrange("a (t m) -> a t m", t=4),
+        qb = {}
+
+        def product_tile(i, which, dest):
+            if i not in dest:
+                dest[i] = keep.tile([P, 4, P], F32, name="%s_%d" % (which, i))
+            return dest[i]
+
+        def table(i, which, c0, c1):
+            return tab[(which, i // H)][:, P * c0 : P * c1].rearrange("a (t m) -> a t m", m=P)
+
+        def product(i, which, dest, c0, c1):
+            nc.vector.scalar_tensor_tensor(out=product_tile(i, which, dest)[:, c0:c1, :],
+                                           in0=acc[i][:].rearrange("a (m t) -> a t m", t=4)[:, c0:c1, :],
+                                           scalar=bias[:, i % H : i % H + 1], in1=table(i, which, c0, c1),
                                            op0=ALU.add, op1=ALU.mult)
 
-        def product_cos(i):
-            product(i, "cos", t1)
+        def products(i, c0=0, c1=4):
+            product(i, "cos", t1, c0, c1)
+            product(i, "sin", t2, c0, c1)
 
-        def product_sin(i):
-            product(i, "sin", t2)
+        def empty_with_bias(i):
+            qb[i] = keep.tile([P, 4, P], F32, name="qb_%d" % i)
+            nc.scalar.activation(out=qb[i][:], in_=acc[i][:].rearrange("a (m t) -> a t m", t=4), func=ACT.Identity,
+                                 bias=bias[:, i % H : i % H + 1], scale=1.0)
 
-        def turn_and_add(i):
-            t = ps_o.tile([P, 4, P], F32, name="o")
-            for c in range(4):
-                nc.tensor.matmul(t[:, c, :], lhsT=t1[i][:, c, :], rhs=ident[:], is_transpose=True, start=True, stop=False)
-                nc.tensor.matmul(t[:, c, :], lhsT=t2[i][:, c, :], rhs=swp[:], is_transpose=True, start=False, stop=True)
-            o[i] = t
+        def products_g(i, c0=0, c1=4):
+            for which, dest in (("cos", t1), ("sin", t2)):
+                nc.gpsimd.tensor_tensor(out=product_tile(i, which, dest)[:, c0:c1, :], in0=qb[i][:, c0:c1, :],
+                                        in1=table(i, which, c0, c1), op=ALU.mult)
 
-        def empty_and_store(i):
+        def turn_and_add(i, c0=0, c1=4):
+            if i not in o:
+                o[i] = ps_o.tile([P, 4, P], F32, name="o")
+            for c in range(c0, c1):
+                nc.tensor.matmul(o[i][:, c, :], lhsT=t1[i][:, c, :], rhs=ident[:], is_transpose=True, start=True, stop=False)
+                nc.tensor.matmul(o[i][:, c, :], lhsT=t2[i][:, c, :], rhs=swp[:], is_transpose=True, start=False, stop=True)
+
+        def empty_and_store(i, c0=0, c1=4):
             b, h = divmod(i, H)
-            res[i] = keep.tile([P, 4, P], F32, name="res_%d" % i)
-            nc.scalar.copy(out=res[i][:], in_=o[i][:])
-            nc.sync.dma_start(out=out_0[h, b].rearrange("(m t) d -> m t d", t=4), in_=res[i][:])
+            if i not in res:
+                res[i] = keep.tile([P, 4, P], F32, name="res_%d" % i)
+            nc.scalar.copy(out=res[i][:, c0:c1, :], in_=o[i][:, c0:c1, :])
+            nc.sync.dma_start(out=out_0[h, b].rearrange("(m t) d -> m t d", t=4)[:, c0:c1, :], in_=res[i][:, c0:c1, :])
 
-        def row_amax(i):
-            nc.vector.tensor_reduce(out=amax[:, i, :], in_=res[i][:], axis=AX.X, op=ALU.max, apply_absolute_value=True)
+        def row_amax(i, c0=0, c1=4):
+            nc.vector.tensor_reduce(out=amax[:, i, c0:c1], in_=res[i][:, c0:c1, :], axis=AX.X, op=ALU.max,
+                                    apply_absolute_value=True)
 
         def row_reciprocal(i0, i1):
             nc.vector.reciprocal(out=rcp[:, i0:i1, :].rearrange("p i c -> p (i c)"),
@@ -331,8 +345,7 @@ def tile_attentionmodule_pa_kernel(tc, x, x_mask, Wq, bq, out_0, out_1):
         x_group_s(1, 1, 256, 384)
         x_group_s(1, 1, 384, 512)
 
-        product_cos(0)
-        product_sin(0)
+        products(0)
         w_quantize(3)
         open_gate()
         x_group_g(1, 0, 0, 256)
@@ -341,67 +354,61 @@ def tile_attentionmodule_pa_kernel(tc, x, x_mask, Wq, bq, out_0, out_1):
         empty_and_store(0)
         project(3)
         tab_abs(1)
-        product_cos(1)
-        product_sin(1)
+        products(1)
         turn_and_add(1)
         empty_and_store(1)
         tab_sin(1)
         tab_cos(1)
-        product_cos(2)
-        product_sin(2)
+        products(2)
         turn_and_add(2)
         empty_and_store(2)
-        product_cos(3)
-        product_sin(3)
+        products(3)
         turn_and_add(3)
         empty_and_store(3)
         x_quantize(1, 0)
         x_quantize(1, 1)
         project(4)
         project(5)
+        project(6)
         row_amax(0)
         row_amax(1)
-        product_cos(4)
+        empty_with_bias(4)
         row_reciprocal(0, 2)
         row_factor("g", 0, 2)
-        product_sin(4)
-        turn_and_add(4)
-        project(6)
+        products_g(4)
         project(7)
+        products(5)
+        turn_and_add(5)
         cast_s(0)
         store_bytes(0)
         row_amax(2)
         cast_s(1)
         store_bytes(1)
-        empty_and_store(4)
-        product_cos(5)
         row_reciprocal(2, 3)
-        row_factor("g", 2, 3)
-        product_sin(5)
-        turn_and_add(5)
+        row_factor("s", 2, 3)
+        products(6)
+        turn_and_add(4)
+        turn_and_add(6)
+        empty_and_store(5)
         row_amax(3)
         cast_s(2)
         store_bytes(2)
-        empty_and_store(5)
-        product_cos(6)
+        empty_and_store(4)
         row_reciprocal(3, 4)
         row_factor("g", 3, 4)
-        product_sin(6)
-        turn_and_add(6)
+        products(7)
+        turn_and_add(7)
         cast_s(3)
         store_bytes(3)
         empty_and_store(6)
-        product_cos(7)
-        product_sin(7)
-        turn_and_add(7)
-        row_amax(4)
         row_amax(5)
-        row_reciprocal(4, 5)
-        row_factor("g", 4, 5)
+        row_amax(4)
+        row_reciprocal(4, 6)
+        row_factor("g", 4, 6)
         empty_and_store(7)
         row_amax(6)
-        row_reciprocal(5, 7)
-        row_factor("g", 5, 7)
+        row_reciprocal(6, 7)
+        row_factor("g", 6, 7)
         cast_s(4)
         store_bytes(4)
         row_amax(7)

@@ -367,58 +367,63 @@ def tile_attentionmodule_pa_kernel(tc, x, x_mask, Wq, bq, out_0, out_1):
         empty_and_store(3)
         x_quantize(1, 0)
         x_quantize(1, 1)
-        project(4)
         project(5)
+        project(4)
         project(6)
         row_amax(0)
         row_amax(1)
         empty_with_bias(4)
+        product(5, "cos", t1, 0, 4)
         row_reciprocal(0, 2)
         row_factor("g", 0, 2)
         products_g(4)
+        product(5, "sin", t2, 0, 4)
         project(7)
-        products(5)
         turn_and_add(5)
         cast_s(0)
         store_bytes(0)
         row_amax(2)
         cast_s(1)
         store_bytes(1)
+        product(6, "cos", t1, 0, 4)
         row_reciprocal(2, 3)
         row_factor("s", 2, 3)
-        products(6)
-        turn_and_add(4)
+        product(6, "sin", t2, 0, 4)
         turn_and_add(6)
         empty_and_store(5)
         row_amax(3)
         cast_s(2)
         store_bytes(2)
-        empty_and_store(4)
+        turn_and_add(4)
+        empty_and_store(6)
+        product(7, "cos", t1, 0, 4)
         row_reciprocal(3, 4)
         row_factor("g", 3, 4)
-        products(7)
+        product(7, "sin", t2, 0, 4)
         turn_and_add(7)
         cast_s(3)
         store_bytes(3)
-        empty_and_store(6)
+        empty_and_store(4)
         row_amax(5)
-        row_amax(4)
-        row_reciprocal(4, 6)
-        row_factor("g", 4, 6)
-        empty_and_store(7)
         row_amax(6)
+        row_reciprocal(5, 6)
+        row_factor("g", 5, 6)
+        empty_and_store(7)
+        row_amax(4)
         row_reciprocal(6, 7)
+        row_reciprocal(4, 5)
         row_factor("g", 6, 7)
-        cast_s(4)
-        store_bytes(4)
-        row_amax(7)
-        cast_v(6, 0, 2)
+        row_factor("g", 4, 5)
         cast_s(5)
         store_bytes(5)
+        row_amax(7)
+        cast_v(6, 0, 2)
+        cast_s(4)
+        store_bytes(4)
         row_reciprocal(7, 8)
         cast_v(6, 2, 4)
         store_bytes(6)
         row_factor("v", 7, 8)
-        cast_v(7, 0, 2)
-        cast_s(7, 2, 4)
+        cast_v(7, 0, 3)
+        cast_s(7, 3, 4)
         store_bytes(7)

@@ -401,29 +401,29 @@ def tile_attentionmodule_pa_kernel(tc, x, x_mask, Wq, bq, out_0, out_1):
         row_factor("g", 3, 4)
         product(7, "sin", t2, 0, 4)
         turn_and_add(7)
-        cast_s(3)
-        store_bytes(3)
         empty_and_store(4)
         row_amax(5)
+        cast_v(3)
+        store_bytes(3)
+        empty_and_store(7)
         row_amax(6)
         row_reciprocal(5, 6)
         row_factor("g", 5, 6)
-        empty_and_store(7)
         row_amax(4)
         row_reciprocal(6, 7)
-        row_reciprocal(4, 5)
         row_factor("g", 6, 7)
-        row_factor("g", 4, 5)
-        cast_s(5)
-        store_bytes(5)
         row_amax(7)
-        cast_v(6, 0, 2)
-        cast_s(4)
-        store_bytes(4)
+        row_reciprocal(4, 5)
+        row_factor("g", 4, 5)
+        cast_v(5)
+        store_bytes(5)
         row_reciprocal(7, 8)
-        cast_v(6, 2, 4)
+        cast_v(6)
         store_bytes(6)
         row_factor("v", 7, 8)
-        cast_v(7, 0, 3)
+        cast_s(4, 2, 4)
+        cast_v(4, 0, 2)
+        store_bytes(4)
         cast_s(7, 3, 4)
+        cast_v(7, 0, 3)
         store_bytes(7)

import math
from contextlib import ExitStack

import concourse.mybir as mybir
from concourse.masks import make_identity

B, T, DM, A, H, HD = 2, 512, 1024, 512, 4, 128
FLOPS = 2 * B * T * DM * A

F32 = mybir.dt.float32
BF16 = mybir.dt.bfloat16
I32 = mybir.dt.int32
U32 = mybir.dt.uint32
U8 = mybir.dt.uint8
FP8X4 = mybir.dt.float8_e4m3fn_x4
FP8 = mybir.dt.float8_e4m3fn
ALU = mybir.AluOpType
ACT = mybir.ActivationFunctionType
AX = mybir.AxisListType

P = 128
TILES = B * H
TWO_PI = 2.0 * math.pi
THETA0_TURNS = 10.0 / TWO_PI
THETA_RATIO = 10000.0 ** (-2.0 / HD)


def tile_attentionmodule_pa_kernel(tc, x, x_mask, Wq, bq, out_0, out_1):
    nc = tc.nc
    with ExitStack() as ctx:
        keep = ctx.enter_context(tc.tile_pool(name="keep", bufs=1))
        ps_acc = ctx.enter_context(tc.psum_pool(name="ps_acc", bufs=3))
        ps_o = ctx.enter_context(tc.psum_pool(name="ps_o", bufs=4))
        ps_misc = ctx.enter_context(tc.psum_pool(name="ps_misc", bufs=1))
        ctx.enter_context(tc.manual_schedule())

        mk = keep.tile([P, B, 4], BF16, name="mk")
        nc.scalar.dma_start(out=mk[:], in_=x_mask.rearrange("b o (p e) -> p (b o) e", e=4))
        bias = keep.tile([P, H], BF16, name="bias")
        with nc.allow_non_contiguous_dma(reason="one bias value to a partition"):
            nc.scalar.dma_start(out=bias[:], in_=bq.rearrange("(h a) -> a h", a=P))

        wraw = {}
        xraw = {}

        def load_w(h):
            t = keep.tile([P, DM], BF16, name="wraw%d" % h)
            nc.sync.dma_start(out=t[:], in_=Wq[P * h : P * (h + 1), :])
            wraw[h] = t

        def load_x(b, g):
            t = keep.tile([P, 4, T], BF16, name="xraw%d%d" % (b, g))
            nc.sync.dma_start(out=t[:], in_=x[b, 512 * g : 512 * (g + 1), :].rearrange("(p j) t -> p j t", j=4))
            xraw[(b, g)] = t

        load_w(0)
        load_x(0, 0)
        load_x(0, 1)
        load_w(1)
        load_w(2)
        load_w(3)
        load_x(1, 0)
        load_x(1, 1)

        zero = keep.tile([P, 1], F32, name="zero")
        nc.vector.memset(zero[:], 0.0)
        warm = keep.tile([P, 1], F32, name="warm")
        nc.scalar.activation(out=warm[:], in_=zero[:], func=ACT.Sin)
        ones = keep.tile([P, P], BF16, name="ones")
        ident = keep.tile([P, P], F32, name="ident")
        make_identity(nc, ident[:])
        tpos = keep.tile([P, T], F32, name="tpos")
        nc.gpsimd.iota(tpos[:], pattern=[[1, 4], [4, 128]], base=0, channel_multiplier=0,
                       allow_small_or_imprecise_dtypes=True)
        swp = keep.tile([P, P], F32, name="swp")
        nc.scalar.copy(out=swp[:, 0:64], in_=ident[:, 64:128])
        nc.scalar.copy(out=swp[:, 64:128], in_=ident[:, 0:64])

        unit = keep.tile([P, 64], F32, name="unit")
        nc.vector.memset(unit[:], 1.0)
        none = keep.tile([P, 64], F32, name="none")
        nc.vector.memset(none[:], 0.0)
        ratio = keep.tile([P, 64], F32, name="ratio")
        nc.vector.tensor_scalar(out=ratio[:], in0=unit[:], scalar1=THETA_RATIO, scalar2=None, op0=ALU.mult)
        th = keep.tile([P, P], F32, name="th")
        nc.vector.tensor_tensor_scan(out=th[:, 0:64], data0=ratio[:], data1=none[:], initial=THETA0_TURNS / THETA_RATIO,
                                     op0=ALU.mult, op1=ALU.add)
        nc.vector.tensor_tensor_scan(out=th[:, 64:128], data0=ratio[:], data1=none[:], initial=-THETA0_TURNS / THETA_RATIO,
                                     op0=ALU.mult, op1=ALU.add)
        nc.vector.memset(ones[:], 1.0)
        wide = keep.tile([P, T], BF16, name="wide")
        nc.scalar.copy(out=wide[:], in_=ones[:, 0:1].to_broadcast([P, T]))
        half_pi = keep.tile([P, 1], F32, name="half_pi")
        nc.vector.tensor_scalar(out=half_pi[:], in0=unit[:, 0:1], scalar1=0.5 * math.pi, scalar2=None, op0=ALU.mult)

        idle_sums = ps_acc.tile([P, T], F32, name="acc")

        def raise_clock(passes, moving, width):
            for k in range(passes):
                nc.tensor.matmul(idle_sums[:, 0:width], lhsT=ones[:], rhs=moving, start=True, stop=True)

        misc = ps_misc.tile([P, 256], F32, name="misc")
        nc.tensor.transpose(misc[:, 0:128], th[:], ident[:])
        raise_clock(8, ones[:], P)
        for e in range(4):
            nc.tensor.matmul(misc[:, 128:130], lhsT=ones[:], rhs=mk[:, :, e], start=(e == 0), stop=(e == 3))
        rn = keep.tile([P, B], F32, name="rn")
        gate = keep.tile([P, 1], F32, name="gate")
        tth = keep.tile([P, T], F32, name="tth")

        def token_times_theta():
            nc.vector.tensor_scalar(out=tth[:], in0=tpos[:], scalar1=misc[:, 0:1], scalar2=None, op0=ALU.mult)

        def one_over_length():
            nc.vector.reciprocal(out=rn[:], in_=misc[:, 128:130])

        def open_gate():
            nc.vector.memset(gate[:], 1.0)

        tab = {}

        def tab_ks(b):
            t = keep.tile([P, T], I32, name="ks%d" % b)
            nc.vector.tensor_scalar(out=t[:], in0=tth[:], scalar1=rn[:, b : b + 1], scalar2=0.0, op0=ALU.mult, op1=ALU.add)
            tab[("ks", b)] = t

        def tab_vs(b):
            t = keep.tile([P, T], F32, name="vs%d" % b)
            nc.vector.scalar_tensor_tensor(out=t[:], in0=tth[:], scalar=rn[:, b : b + 1], in1=tab[("ks", b)][:],
                                           op0=ALU.mult, op1=ALU.subtract)
            tab[("vs", b)] = t

        def tab_sin(b):
            t = keep.tile([P, T], F32, name="sin%d" % b)
            nc.scalar.activation(out=t[:], in_=tab[("vs", b)][:], func=ACT.Sin, scale=TWO_PI)
            tab[("sin", b)] = t

        def tab_abs(b):
            t = keep.tile([P, T], F32, name="abs%d" % b)
            nc.scalar.activation(out=t[:], in_=tab[("vs", b)][:], func=ACT.Abs)
            tab[("abs", b)] = t

        def tab_cos(b):
            t = keep.tile([P, T], F32, name="cos%d" % b)
            nc.scalar.activation(out=t[:], in_=tab[("abs", b)][:], func=ACT.Sin, scale=-TWO_PI, bias=half_pi[:, 0:1])
            tab[("cos", b)] = t

        wt = {}
        wgrp = {}
        w_codes = {}
        w_scales = {}

        def w_transpose(h):
            words = wraw[h][:].bitcast(F32)
            t = ps_o.tile([P, 2, 2, P], F32, name="o")
            for g in range(2):
                for u in range(2):
                    nc.tensor.transpose(t[:, g, u, :], words[:, 256 * g + u : 256 * (g + 1) : 2], ident[:])
            wt[h] = t

        def w_copy(h):
            grp = keep.tile([P, 1024], BF16, name="wgrp%d" % h, align_bytes=64)
            nc.scalar.copy(out=grp[:].bitcast(F32).rearrange("p (g a u) -> p g a u", g=2, u=2),
                           in_=wt[h][:].rearrange("p g u a -> p g a u"))
            wgrp[h] = grp

        def w_quantize(h):
            codes = keep.tile([P, 256], U32, name="wcod%d" % h, align_bytes=64)
            scl = keep.tile([P, 256], U8, name="wscl%d" % h, align_bytes=64)
            nc.vector.quantize_mx(out=codes[:].bitcast(FP8X4), scales=scl[:], in_=wgrp[h][:])
            w_codes[h] = codes
            w_scales[h] = scl

        xgrp = {}
        for b in range(B):
            for g in range(2):
                xgrp[(b, g)] = keep.tile([P, T, 4], BF16, name="xgrp%d%d" % (b, g), align_bytes=64)
        x_codes = {}
        x_scales = {}

        def x_group_v(b, g, c0, c1):
            nc.vector.tensor_copy(out=xgrp[(b, g)][:, c0:c1, :].rearrange("p (c i) j -> p c j i", i=4),
                                  in_=xraw[(b, g)][:, :, c0:c1].rearrange("p j (c i) -> p c j i", i=4))

        def x_group_s(b, g, c0, c1):
            nc.scalar.copy(out=xgrp[(b, g)][:, c0:c1, :].rearrange("p (c i) j -> p c j i", i=4),
                           in_=xraw[(b, g)][:, :, c0:c1].rearrange("p j (c i) -> p c j i", i=4))

        def x_group_g(b, g, c0, c1):
            nc.gpsimd.tensor_scalar(out=xgrp[(b, g)][:, c0:c1, :], in0=xraw[(b, g)][:, :, c0:c1].rearrange("p j t -> p t j"),
                                    scalar1=gate[:], scalar2=0.0, op0=ALU.mult, op1=ALU.add)

        def x_quantize(b, g):
            codes = keep.tile([P, T], U32, name="xcod%d%d" % (b, g), align_bytes=64)
            scl = keep.tile([P, T], U8, name="xscl%d%d" % (b, g), align_bytes=64)
            nc.vector.quantize_mx(out=codes[:].bitcast(FP8X4), scales=scl[:],
                                  in_=xgrp[(b, g)][:].rearrange("p t j -> p (t j)"))
            x_codes[(b, g)] = codes
            x_scales[(b, g)] = scl

        acc = {}
        t1 = {}
        t2 = {}
        o = {}
        res = {}
        amax = keep.tile([P, TILES, 4], F32, name="amax")
        rcp = keep.tile([P, TILES, 4], F32, name="rcp")
        fac = {}
        for e in ("g", "s", "v"):
            fac[e] = keep.tile([P, TILES, 4], F32, name="fac_" + e)
        fac_of = {}

        def project(i):
            b, h = divmod(i, H)
            acc[i] = ps_acc.tile([P, T], F32, name="acc")
            for g in range(2):
                nc.tensor.matmul_mx(
                    out=acc[i][:],
                    lhsT=w_codes[h][:, P * g : P * (g + 1)].bitcast(FP8X4),
                    lhsT_scale=w_scales[h][:, P * g : P * (g + 1)],
                    rhs=x_codes[(b, g)][:].bitcast(FP8X4),
                    rhs_scale=x_scales[(b, g)][:],
                    start=(g == 0),
                    stop=(g == 1),
                )

        qb = {}

        def product_tile(i, which, dest):
            if i not in dest:
                dest[i] = keep.tile([P, 4, P], F32, name="%s_%d" % (which, i))
            return dest[i]

        def table(i, which, c0, c1):
            return tab[(which, i // H)][:, P * c0 : P * c1].rearrange("a (t m) -> a t m", m=P)

        def product(i, which, dest, c0, c1):
            nc.vector.scalar_tensor_tensor(out=product_tile(i, which, dest)[:, c0:c1, :],
                                           in0=acc[i][:].rearrange("a (m t) -> a t m", t=4)[:, c0:c1, :],
                                           scalar=bias[:, i % H : i % H + 1], in1=table(i, which, c0, c1),
                                           op0=ALU.add, op1=ALU.mult)

        def products(i, c0=0, c1=4):
            product(i, "cos", t1, c0, c1)
            product(i, "sin", t2, c0, c1)

        def empty_with_bias(i):
            qb[i] = keep.tile([P, 4, P], F32, name="qb_%d" % i)
            nc.scalar.activation(out=qb[i][:], in_=acc[i][:].rearrange("a (m t) -> a t m", t=4), func=ACT.Identity,
                                 bias=bias[:, i % H : i % H + 1], scale=1.0)

        def products_g(i, c0=0, c1=4):
            for which, dest in (("cos", t1), ("sin", t2)):
                nc.gpsimd.tensor_tensor(out=product_tile(i, which, dest)[:, c0:c1, :], in0=qb[i][:, c0:c1, :],
                                        in1=table(i, which, c0, c1), op=ALU.mult)

        def turn_and_add(i, c0=0, c1=4):
            if i not in o:
                o[i] = ps_o.tile([P, 4, P], F32, name="o")
            for c in range(c0, c1):
                nc.tensor.matmul(o[i][:, c, :], lhsT=t1[i][:, c, :], rhs=ident[:], is_transpose=True, start=True, stop=False)
                nc.tensor.matmul(o[i][:, c, :], lhsT=t2[i][:, c, :], rhs=swp[:], is_transpose=True, start=False, stop=True)

        def empty_and_store(i, c0=0, c1=4):
            b, h = divmod(i, H)
            if i not in res:
                res[i] = keep.tile([P, 4, P], F32, name="res_%d" % i)
            nc.scalar.copy(out=res[i][:, c0:c1, :], in_=o[i][:, c0:c1, :])
            nc.sync.dma_start(out=out_0[h, b].rearrange("(m t) d -> m t d", t=4)[:, c0:c1, :], in_=res[i][:, c0:c1, :])

        def row_amax(i, c0=0, c1=4):
            nc.vector.tensor_reduce(out=amax[:, i, c0:c1], in_=res[i][:, c0:c1, :], axis=AX.X, op=ALU.max,
                                    apply_absolute_value=True)

        def row_reciprocal(i0, i1):
            nc.vector.reciprocal(out=rcp[:, i0:i1, :].rearrange("p i c -> p (i c)"),
                                 in_=amax[:, i0:i1, :].rearrange("p i c -> p (i c)"))

        def row_factor(e, i0, i1):
            dst = fac[e][:, i0:i1, :].rearrange("p i c -> p (i c)")
            src = rcp[:, i0:i1, :].rearrange("p i c -> p (i c)")
            if e == "g":
                nc.gpsimd.tensor_scalar(out=dst, in0=src, scalar1=448.0, scalar2=0.0, op0=ALU.mult, op1=ALU.add)
            elif e == "s":
                nc.scalar.activation(out=dst, in_=src, func=ACT.Copy, scale=448.0)
            else:
                nc.vector.tensor_scalar(out=dst, in0=src, scalar1=448.0, scalar2=None, op0=ALU.mult)
            for i in range(i0, i1):
                fac_of[i] = fac[e]

        o8 = {}

        def bytes_tile(i):
            if i not in o8:
                o8[i] = keep.tile([P, 4, P], FP8, name="o8_%d" % i)
            return o8[i]

        def cast_s(i, c0=0, c1=4):
            for c in range(c0, c1):
                nc.scalar.activation(out=bytes_tile(i)[:, c, :], in_=res[i][:, c, :], func=ACT.Identity,
                                     scale=fac_of[i][:, i, c : c + 1], bias=zero[:, 0:1], saturate=False)

        def cast_v(i, c0=0, c1=4):
            for c in range(c0, c1):
                nc.vector.tensor_scalar(out=bytes_tile(i)[:, c, :], in0=res[i][:, c, :], scalar1=fac_of[i][:, i, c : c + 1],
                                        scalar2=None, op0=ALU.mult, saturate=False)

        def store_bytes(i):
            b, h = divmod(i, H)
            nc.sync.dma_start(out=out_1[h, b].rearrange("(m t) d -> m (t d)", t=4),
                              in_=o8[i][:].rearrange("p t d -> p (t d)").bitcast(U8))

        token_times_theta()
        one_over_length()
        tab_ks(0)
        tab_ks(1)
        w_transpose(0)
        raise_clock(4, wide[:], T)
        w_copy(0)
        tab_vs(0)
        x_group_s(0, 0, 352, 512)
        tab_sin(0)
        x_group_v(0, 0, 0, 352)
        w_quantize(0)
        x_group_s(0, 1, 352, 512)
        tab_abs(0)
        x_group_v(0, 1, 0, 352)
        w_transpose(1)
        w_transpose(2)
        w_transpose(3)
        w_copy(1)
        w_copy(2)
        tab_cos(0)
        w_copy(3)
        x_quantize(0, 0)
        x_quantize(0, 1)
        project(0)
        tab_vs(1)
        w_quantize(1)
        w_quantize(2)
        project(1)
        project(2)
        x_group_s(1, 0, 256, 384)
        x_group_s(1, 0, 384, 512)
        x_group_s(1, 1, 256, 384)
        x_group_s(1, 1, 384, 512)

        products(0)
        w_quantize(3)
        open_gate()
        x_group_g(1, 0, 0, 256)
        x_group_g(1, 1, 0, 256)
        turn_and_add(0)
        empty_and_store(0)
        project(3)
        tab_abs(1)
        products(1)
        turn_and_add(1)
        empty_and_store(1)
        tab_sin(1)
        tab_cos(1)
        products(2)
        turn_and_add(2)
        empty_and_store(2)
        products(3)
        turn_and_add(3)
        empty_and_store(3)
        x_quantize(1, 0)
        x_quantize(1, 1)
        project(5)
        project(4)
        project(6)
        row_amax(0)
        row_amax(1)
        empty_with_bias(4)
        product(5, "cos", t1, 0, 4)
        row_reciprocal(0, 2)
        row_factor("g", 0, 2)
        products_g(4)
        product(5, "sin", t2, 0, 4)
        project(7)
        turn_and_add(5)
        cast_s(0)
        store_bytes(0)
        row_amax(2)
        cast_s(1)
        store_bytes(1)
        product(6, "cos", t1, 0, 4)
        row_reciprocal(2, 3)
        row_factor("s", 2, 3)
        product(6, "sin", t2, 0, 4)
        turn_and_add(6)
        empty_and_store(5)
        row_amax(3)
        cast_s(2)
        store_bytes(2)
        turn_and_add(4)
        empty_and_store(6)
        product(7, "cos", t1, 0, 4)
        row_reciprocal(3, 4)
        row_factor("g", 3, 4)
        product(7, "sin", t2, 0, 4)
        turn_and_add(7)
        empty_and_store(4)
        row_amax(5)
        cast_v(3)
        store_bytes(3)
        empty_and_store(7)
        row_amax(6)
        row_reciprocal(5, 6)
        row_factor("g", 5, 6)
        row_amax(4)
        row_reciprocal(6, 7)
        row_factor("g", 6, 7)
        row_amax(7)
        row_reciprocal(4, 5)
        row_factor("g", 4, 5)
        cast_v(5)
        store_bytes(5)
        row_reciprocal(7, 8)
        cast_v(6)
        store_bytes(6)
        row_factor("v", 7, 8)
        cast_s(4, 2, 4)
        cast_v(4, 0, 2)
        store_bytes(4)
        cast_s(7, 3, 4)
        cast_v(7, 0, 3)
        store_bytes(7)
